import numpy as np
import ml_dtypes


def mxq(x, axis, fmt="e4m3"):
    dtype, down = {"e4m3": (ml_dtypes.float8_e4m3fn, 7), "e5m2": (ml_dtypes.float8_e5m2, 14)}[fmt]
    v = np.moveaxis(np.asarray(x, np.float32).astype(ml_dtypes.bfloat16).astype(np.float64), axis, -1)
    blocks = v.reshape(v.shape[:-1] + (-1, 32))
    amax = np.abs(blocks).max(-1, keepdims=True)
    byte = np.maximum(np.where(amax > 0, np.frexp(amax)[1] - 1 + 127, 0) - down, 1)
    scale = np.exp2(byte - 127.0)
    codes = (blocks / scale).astype(np.float32).astype(dtype).astype(np.float64)
    return np.moveaxis((codes * scale).reshape(v.shape), -1, axis)


WIDE = False


def mx_kscale(k):
    if not WIDE:
        return np.ones(k)
    levels = np.array([10, -10, 5, -5, 0])
    if k % 512:
        return np.exp2(np.random.permutation(np.resize(levels, k // 32))).repeat(32)
    a = np.empty((k // 512, 16))
    for p in range(k // 512):
        a[p, :8] = np.random.permutation(np.resize(levels, 8))
        for g in range(8):
            far = levels[np.abs(levels - a[p, g]) >= 10]
            a[p, g + 8] = far[np.random.randint(len(far))]
    return np.exp2(a.ravel()).repeat(32)


BF16 = ml_dtypes.bfloat16


def bf(x):
    return np.asarray(x, np.float32).astype(BF16)


def f64(x):
    return np.asarray(x).astype(np.float64)


B, S, D, H, DK, F = 2, 2048, 512, 4, 128, 256
HD = H * DK
EPS = 1e-6


def rmsnorm(v, g):
    return v / np.sqrt(np.mean(v * v, axis=-1, keepdims=True) + EPS) * g


def silu(v):
    return v / (1.0 + np.exp(-v))


def draw0():
    s, t = mx_kscale(HD), mx_kscale(D)
    return {"x": bf(np.random.standard_normal((B, S, D))),
            "ao": bf(np.random.standard_normal((B, H, S, DK)) * 0.3 * s.reshape(H, 1, DK)),
            "wo": bf(np.random.standard_normal((HD, D)) * 1.5 / np.sqrt(HD) / s[:, None]),
            "bo": bf(np.random.standard_normal(D) * 0.1),
            "g2": bf((1.0 + 0.1 * np.random.standard_normal(D)) * t),
            "w1": bf(np.random.standard_normal((D, F)) / np.sqrt(D) / t[:, None]),
            "w3": bf(np.random.standard_normal((D, F)) / np.sqrt(D) / t[:, None])}


def core(x, ao, wo, bo, g2, w1, w3):
    a = f64(ao).transpose(0, 2, 1, 3).reshape(B, S, HD)
    x1 = f64(x) + ((mxq(a, 2, "e4m3") @ mxq(f64(wo), 0, "e4m3")) + f64(bo))
    n = mxq(rmsnorm(x1, f64(g2)), 2, "e4m3")
    h = silu(n @ mxq(f64(w1), 0, "e4m3")) * (n @ mxq(f64(w3), 0, "e4m3"))
    return x1, h


def e4m3fn_bytes(y):
    return np.clip(np.asarray(y, np.float64), -448.0, 448.0).astype(np.float32).astype(ml_dtypes.float8_e4m3fn).view(np.uint8)


def e4m3fn_values(b):
    return np.asarray(b, np.uint8).view(ml_dtypes.float8_e4m3fn).astype(np.float64)


def setup_inputs():
    d = draw0()
    x0 = np.asarray(d['wo']).astype(np.float64)
    s = (np.max(np.abs(x0), axis=(1,), keepdims=True) / 448.0).astype(np.float32)
    out = {}
    for k, v in d.items():
        if k == 'wo':
            out['wo_bytes'] = e4m3fn_bytes(x0 / s.astype(np.float64))
            out['wo_scale'] = s
        else:
            out[k] = v
    return out


def reference(x, ao, wo_bytes, wo_scale, bo, g2, w1, w3):
    return core(x, ao, e4m3fn_values(wo_bytes) * wo_scale.astype(np.float64), bo, g2, w1, w3)

@@ -1,0 +1,285 @@
+from contextlib import ExitStack
+
+import concourse.mybir as mybir
+from concourse.masks import make_identity
+
+F32 = mybir.dt.float32
+BF16 = mybir.dt.bfloat16
+U32 = mybir.dt.uint32
+U8 = mybir.dt.uint8
+FP8 = mybir.dt.float8_e4m3fn
+FP8X4 = mybir.dt.float8_e4m3fn_x4
+ACT = mybir.ActivationFunctionType
+ALU = mybir.AluOpType
+
+B, S, D, H, DK, F = 2, 2048, 512, 4, 128, 256
+EPS = 1e-6
+FLOPS = 2 * B * S * (H * DK * D + D * 2 * F)
+
+P = 128
+J = 4
+I = S // P
+PAIRS_B = I // 2
+NP = B * PAIRS_B
+CHUNKS = ((0, 0, 2), (0, 2, 2), (0, 4, 4), (0, 8, 8), (1, 0, 8), (1, 8, 8))
+
+
+def tile_transformerblock_pb_t_kernel(tc, x, ao, wo_bytes, wo_scale, bo, g2, w1, w3, out_0, out_1):
+    nc = tc.nc
+    with ExitStack() as ctx:
+        const = ctx.enter_context(tc.tile_pool(name="const", bufs=1))
+        loads = ctx.enter_context(tc.tile_pool(name="loads", bufs=1))
+        res = ctx.enter_context(tc.tile_pool(name="res", bufs=NP))
+        work = ctx.enter_context(tc.tile_pool(name="work", bufs=3))
+        psum = ctx.enter_context(tc.psum_pool(name="psum", bufs=2))
+        psum1 = ctx.enter_context(tc.psum_pool(name="psum1", bufs=1))
+        ctx.enter_context(tc.manual_schedule())
+
+        bo_row = const.tile([P, D], BF16)
+        nc.vector.memset(bo_row[:], 0.0)
+        warm = const.tile([P, 1], F32)
+        nc.vector.memset(warm[:], 0.0)
+        ones = const.tile([P, P], BF16)
+        nc.vector.memset(ones[:], 1.0)
+        neg_half = const.tile([P, 2], F32)
+        nc.gpsimd.memset(neg_half[:], -0.5)
+        ident = const.tile([P, P], F32)
+        make_identity(nc, ident[:])
+
+        wsc = const.tile([P, J], F32)
+        nc.scalar.dma_start(out=wsc[:], in_=wo_scale.rearrange("(p t) o -> p (t o)", t=J))
+        nc.scalar.dma_start(out=bo_row[0:1, :], in_=bo.rearrange("(o n) -> o n", o=1))
+        g2t = const.tile([P, J], BF16)
+        nc.scalar.dma_start(out=g2t[:], in_=g2.rearrange("(p t) -> p t", t=J))
+        warm2 = const.tile([P, 1], F32)
+        nc.scalar.activation(out=warm2[:], in_=warm[:], func=ACT.Silu)
+
+        wob = const.tile([P, J, D], U8, align_bytes=64)
+        nc.sync.dma_start(out=wob[:], in_=wo_bytes.rearrange("(p t) n -> p t n", t=J))
+        ao_t = {}
+        x_t = {}
+
+        def load_ao(c):
+            b, i0, n = CHUNKS[c]
+            t = loads.tile([P, n, H, DK], BF16, name="ao%d" % c, align_bytes=64)
+            src = ao[b].rearrange("h (p i) d -> p i h d", i=I)
+            for i in range(n):
+                nc.sync.dma_start(out=t[:, i, :, :], in_=src[:, i0 + i, :, :])
+                ao_t[b * I + i0 + i] = t[:, i, :, :]
+
+        def load_x(c):
+            b, i0, n = CHUNKS[c]
+            t = loads.tile([P, n, D], BF16, name="x%d" % c, align_bytes=64)
+            nc.sync.dma_start(out=t[:], in_=x[b].rearrange("(p i) d -> p i d", i=I)[:, i0 : i0 + n, :])
+            for i in range(n):
+                x_t[b * I + i0 + i] = t[:, i, :]
+
+        load_ao(0)
+        load_x(0)
+        w_raw = const.tile([P, J, 2 * F], BF16, align_bytes=64)
+        load_ao(1)
+        nc.sync.dma_start(out=w_raw[:, :, 0:F], in_=w1.rearrange("(p j) f -> p j f", j=J))
+        nc.sync.dma_start(out=w_raw[:, :, F : 2 * F], in_=w3.rearrange("(p j) f -> p j f", j=J))
+        load_x(1)
+        for c in range(2, len(CHUNKS)):
+            load_ao(c)
+            load_x(c)
+
+        st = {}
+
+        def t_stage(s):
+            bank = psum.tile([P, 2, 2, P], F32, name="aT_ps")
+            for a in range(2):
+                words = ao_t[2 * s + a].rearrange("p h d -> p (h d)").bitcast(F32)
+                for u in range(2):
+                    nc.tensor.transpose(bank[:, a, u, :], words[:, u : 2 * P : 2], ident[:])
+            st["aT", s] = bank
+
+        def c_stage(s):
+            bank = st["aT", s]
+            g = work.tile([P, 2, P, J], BF16, name="ag", align_bytes=64)
+            nc.scalar.copy(
+                out=g[:].rearrange("p a r j -> p (a r j)").bitcast(F32).rearrange("p (a r u) -> p a r u", a=2, u=2),
+                in_=bank[:].rearrange("p a u r -> p a r u"),
+            )
+            st["ag", s] = g
+
+        def quant(src, name):
+            codes = work.tile([P, 2 * P], U32, name=name + "c", align_bytes=64)
+            scales = work.tile([P, 2 * P], U8, name=name + "s", align_bytes=64)
+            nc.vector.quantize_mx(out=codes[:].bitcast(FP8X4), scales=scales[:], in_=src[:].rearrange("p a r j -> p (a r j)"))
+            return codes, scales
+
+        def qa_stage(s):
+            st["qa", s] = quant(st["ag", s], "qa")
+
+        def y_stage(s):
+            codes, scales = st["qa", s]
+            for a in range(2):
+                y = psum.tile([P, D], F32, name="y_ps")
+                nc.tensor.matmul_mx(
+                    out=y[:],
+                    lhsT=codes[:, a * P : (a + 1) * P].bitcast(FP8X4),
+                    lhsT_scale=scales[:, a * P : (a + 1) * P],
+                    rhs=wo_codes[:].bitcast(FP8X4),
+                    rhs_scale=wo_scales[:],
+                    start=True,
+                    stop=True,
+                )
+                st["y", s, a] = y
+
+        def b_stage(s, a):
+            if a == 0:
+                st["x1", s] = res.tile([P, 2, D], F32, name="x1")
+            nc.gpsimd.tensor_tensor(out=st["x1", s][:, a, :], in0=x_t[2 * s + a], in1=bo_t[:], op=ALU.add)
+
+        def x_stage(s):
+            x1 = st["x1", s]
+            for a in range(2):
+                nc.vector.tensor_tensor(out=x1[:, a, :], in0=st["y", s, a][:], in1=x1[:, a, :], op=ALU.add)
+            b, i0 = s // PAIRS_B, 2 * (s % PAIRS_B)
+            nc.sync.dma_start(out=out_0[b].rearrange("(p i) d -> p i d", i=I)[:, i0 : i0 + 2, :], in_=x1[:])
+
+        def sq_stage(s):
+            ssum = work.tile([P, 2], F32, name="ssum")
+            for a in range(2):
+                junk = work.tile([P, D], BF16, name="junk")
+                nc.scalar.activation(out=junk[:], in_=st["x1", s][:, a, :], func=ACT.Square, accum_out=ssum[:, a : a + 1])
+            st["ssum", s] = ssum
+
+        def r_stage(s):
+            ms = work.tile([P, 2], F32, name="ms")
+            nc.gpsimd.tensor_scalar(out=ms[:], in0=st["ssum", s][:], scalar1=1.0 / D, scalar2=EPS, op0=ALU.mult, op1=ALU.add)
+            rstd = work.tile([P, 2], F32, name="rstd")
+            nc.gpsimd.tensor_tensor(out=rstd[:], in0=ms[:], in1=neg_half[:], op=ALU.pow)
+            st["rstd", s] = rstd
+
+        def n_stage(s):
+            for a in range(2):
+                xn = work.tile([P, J, P], F32, name="xn%d" % a)
+                nc.scalar.activation(
+                    out=xn[:].rearrange("p t q -> p q t"),
+                    in_=st["x1", s][:, a, :].rearrange("p (q t) -> p q t", t=J),
+                    func=ACT.Copy,
+                    scale=st["rstd", s][:, a : a + 1],
+                )
+                st["xn", s, a] = xn
+
+        def nt_stage(s):
+            for a in range(2):
+                bank = psum.tile([P, J, P], F32, name="nT_ps")
+                for t in range(J):
+                    nc.tensor.transpose(bank[:, t, :], st["xn", s, a][:, t, :], ident[:])
+                st["nT", s, a] = bank
+
+        def g2_stage(s):
+            ng = work.tile([P, 2, P, J], BF16, name="ng", align_bytes=64)
+            for a in range(2):
+                nc.vector.tensor_tensor(
+                    out=ng[:, a, :, :],
+                    in0=st["nT", s, a][:].rearrange("p t r -> p r t"),
+                    in1=g2t[:].unsqueeze(1).to_broadcast([P, P, J]),
+                    op=ALU.mult,
+                )
+            st["ng", s] = ng
+
+        def qn_stage(s):
+            st["qn", s] = quant(st["ng", s], "qn")
+
+        def uv_stage(s):
+            codes, scales = st["qn", s]
+            u = psum1.tile([P, 2, F], F32, name="u_ps")
+            v = psum1.tile([P, 2, F], F32, name="v_ps")
+            for a in range(2):
+                for dst, f0 in ((u, 0), (v, F)):
+                    nc.tensor.matmul_mx(
+                        out=dst[:, a, :],
+                        lhsT=codes[:, a * P : (a + 1) * P].bitcast(FP8X4),
+                        lhsT_scale=scales[:, a * P : (a + 1) * P],
+                        rhs=w_codes[:, f0 : f0 + F].bitcast(FP8X4),
+                        rhs_scale=w_scales[:, f0 : f0 + F],
+                        start=True,
+                        stop=True,
+                    )
+            st["uv", s] = (u, v)
+
+        def sl_stage(s):
+            sil = work.tile([P, 2, F], F32, name="sil")
+            nc.scalar.activation(out=sil[:], in_=st["uv", s][0][:], func=ACT.Silu)
+            st["sil", s] = sil
+
+        def ml_stage(s):
+            h = work.tile([P, 2, F], F32, name="h")
+            nc.vector.tensor_tensor(out=h[:], in0=st["uv", s][1][:], in1=st["sil", s][:], op=ALU.mult)
+            b, i0 = s // PAIRS_B, 2 * (s % PAIRS_B)
+            nc.sync.dma_start(out=out_1[b].rearrange("(p i) f -> p i f", i=I)[:, i0 : i0 + 2, :], in_=h[:])
+
+        wide = const.tile([P, J, D], BF16, align_bytes=64)
+        for t in range(J):
+            if t < 3:
+                nc.vector.tensor_scalar(out=wide[:, t, :], in0=wob[:, t, :].bitcast(FP8), scalar1=wsc[:, t : t + 1], scalar2=None, op0=ALU.mult)
+            else:
+                nc.scalar.activation(out=wide[:, t, :], in_=wob[:, t, :].bitcast(FP8), func=ACT.Copy, scale=wsc[:, t : t + 1])
+        bo_ps = psum1.tile([P, D], F32, name="u_ps")
+        nc.tensor.matmul(bo_ps[:], lhsT=ones[:], rhs=bo_row[:], start=True, stop=True)
+        bo_t = const.tile([P, D], BF16)
+        nc.scalar.copy(out=bo_t[:], in_=bo_ps[:])
+        t_stage(0)
+        t_stage(1)
+        c_stage(0)
+        c_stage(1)
+        wo_g = const.tile([P, D, J], BF16, align_bytes=64)
+
+        def interleave(dst, src):
+            nc.vector.tensor_copy(
+                out=dst.rearrange("p (c i) t -> p c t i", i=4), in_=src.rearrange("p t (c i) -> p c t i", i=4)
+            )
+
+        interleave(wo_g[:], wide[:])
+        wo_codes = const.tile([P, D], U32, align_bytes=64)
+        wo_scales = const.tile([P, D], U8, align_bytes=64)
+        qa_stage(0)
+        nc.vector.quantize_mx(out=wo_codes[:].bitcast(FP8X4), scales=wo_scales[:], in_=wo_g[:].rearrange("p n j -> p (n j)"))
+        qa_stage(1)
+        y_stage(0)
+        for s in range(2):
+            for a in range(2):
+                b_stage(s, a)
+        w_g = const.tile([P, 2 * F, J], BF16, align_bytes=64)
+        w_codes = const.tile([P, 2 * F], U32, align_bytes=64)
+        w_scales = const.tile([P, 2 * F], U8, align_bytes=64)
+
+        for s in range(NP + 2):
+            if 0 <= s - 1 < NP:
+                nt_stage(s - 1)
+            if s + 2 < NP:
+                t_stage(s + 2)
+            if 0 <= s - 2:
+                sl_stage(s - 2)
+            if s < NP:
+                x_stage(s)
+                sq_stage(s)
+            if s + 2 < NP:
+                c_stage(s + 2)
+                b_stage(s + 2, 0)
+            if s < NP:
+                r_stage(s)
+                n_stage(s)
+            if s + 2 < NP:
+                b_stage(s + 2, 1)
+            if s + 1 < NP:
+                y_stage(s + 1)
+            if s == 0:
+                interleave(w_g[:], w_raw[:])
+            if 0 <= s - 1 < NP:
+                g2_stage(s - 1)
+            if 0 <= s - 2:
+                ml_stage(s - 2)
+            if 0 <= s - 1 < NP:
+                qn_stage(s - 1)
+            if s + 2 < NP:
+                qa_stage(s + 2)
+            if s == 0:
+                nc.vector.quantize_mx(out=w_codes[:].bitcast(FP8X4), scales=w_scales[:], in_=w_g[:].rearrange("p n j -> p (n j)"))
+            if 0 <= s - 1 < NP:
+                uv_stage(s - 1)

@@ -87,8 +87,10 @@ def tile_transformerblock_pb_t_kernel(tc, x, ao, wo_bytes, wo_scale, bo, g2, w1,
 
         st = {}
 
-        def t_stage(s):
+        def t_stage(s, dummies=1):
             bank = psum.tile([P, 2, 2, P], F32, name="aT_ps")
+            for i in range(dummies):
+                nc.tensor.matmul(bank[:].rearrange("p a u r -> p (a u r)"), lhsT=ones[:], rhs=bo_row[:], start=True, stop=True)
             for a in range(2):
                 words = ao_t[2 * s + a].rearrange("p h d -> p (h d)").bitcast(F32)
                 for u in range(2):
@@ -215,71 +217,73 @@ def tile_transformerblock_pb_t_kernel(tc, x, ao, wo_bytes, wo_scale, bo, g2, w1,
             nc.sync.dma_start(out=out_1[b].rearrange("(p i) f -> p i f", i=I)[:, i0 : i0 + 2, :], in_=h[:])
 
         wide = const.tile([P, J, D], BF16, align_bytes=64)
+        wo_g = const.tile([P, D, J], BF16, align_bytes=64)
+        wo_codes = const.tile([P, D], U32, align_bytes=64)
+        wo_scales = const.tile([P, D], U8, align_bytes=64)
+        w_g = const.tile([P, 2 * F, J], BF16, align_bytes=64)
+        w_codes = const.tile([P, 2 * F], U32, align_bytes=64)
+        w_scales = const.tile([P, 2 * F], U8, align_bytes=64)
+        bo_t = const.tile([P, D], BF16)
+
+        def interleave(copy, dst, src):
+            copy(out=dst.rearrange("p (c i) t -> p c t i", i=4), in_=src.rearrange("p t (c i) -> p c t i", i=4))
+
+        bo_ps = psum1.tile([P, D], F32, name="u_ps")
+        nc.tensor.matmul(bo_ps[:], lhsT=ones[:], rhs=bo_row[:], start=True, stop=True)
+        nc.scalar.copy(out=bo_t[:], in_=bo_ps[:])
         for t in range(J):
             if t < 3:
                 nc.vector.tensor_scalar(out=wide[:, t, :], in0=wob[:, t, :].bitcast(FP8), scalar1=wsc[:, t : t + 1], scalar2=None, op0=ALU.mult)
             else:
                 nc.scalar.activation(out=wide[:, t, :], in_=wob[:, t, :].bitcast(FP8), func=ACT.Copy, scale=wsc[:, t : t + 1])
-        bo_ps = psum1.tile([P, D], F32, name="u_ps")
-        nc.tensor.matmul(bo_ps[:], lhsT=ones[:], rhs=bo_row[:], start=True, stop=True)
-        bo_t = const.tile([P, D], BF16)
-        nc.scalar.copy(out=bo_t[:], in_=bo_ps[:])
-        t_stage(0)
-        t_stage(1)
-        c_stage(0)
-        c_stage(1)
-        wo_g = const.tile([P, D, J], BF16, align_bytes=64)
 
-        def interleave(dst, src):
-            nc.vector.tensor_copy(
-                out=dst.rearrange("p (c i) t -> p c t i", i=4), in_=src.rearrange("p t (c i) -> p c t i", i=4)
-            )
+        CUT = 320
+        for s in range(-3, NP + 3):
+            n0, n1, n2 = s - 1, s - 2, s - 3
 
-        interleave(wo_g[:], wide[:])
-        wo_codes = const.tile([P, D], U32, align_bytes=64)
-        wo_scales = const.tile([P, D], U8, align_bytes=64)
-        qa_stage(0)
-        nc.vector.quantize_mx(out=wo_codes[:].bitcast(FP8X4), scales=wo_scales[:], in_=wo_g[:].rearrange("p n j -> p (n j)"))
-        qa_stage(1)
-        y_stage(0)
-        for s in range(2):
-            for a in range(2):
-                b_stage(s, a)
-        w_g = const.tile([P, 2 * F, J], BF16, align_bytes=64)
-        w_codes = const.tile([P, 2 * F], U32, align_bytes=64)
-        w_scales = const.tile([P, 2 * F], U8, align_bytes=64)
+            def ok(i):
+                return 0 <= i < NP
 
-        for s in range(NP + 2):
-            if 0 <= s - 1 < NP:
-                nt_stage(s - 1)
-            if s + 2 < NP:
-                t_stage(s + 2)
-            if 0 <= s - 2:
-                sl_stage(s - 2)
-            if s < NP:
+            if ok(n1):
+                nt_stage(n1)
+            if ok(n2):
+                sl_stage(n2)
+            if ok(s):
                 x_stage(s)
                 sq_stage(s)
-            if s + 2 < NP:
-                c_stage(s + 2)
-                b_stage(s + 2, 0)
-            if s < NP:
                 r_stage(s)
-                n_stage(s)
-            if s + 2 < NP:
-                b_stage(s + 2, 1)
-            if s + 1 < NP:
+            if s > -3 and ok(s + 2):
+                c_stage(s + 2)
+            if s == -2:
+                interleave(nc.vector.tensor_copy, wo_g[:, 0:CUT, :], wide[:, :, 0:CUT])
+                interleave(nc.scalar.copy, wo_g[:, CUT:D, :], wide[:, :, CUT:D])
+                for i in range(2):
+                    b_stage(i, 0)
+                    b_stage(i, 1)
+            if s >= 0 and ok(s + 1):
                 y_stage(s + 1)
+            if ok(s + 3):
+                t_stage(s + 3)
+            if s >= -1 and ok(s + 3):
+                b_stage(s + 3, 0)
+            if ok(n0):
+                n_stage(n0)
+            if s >= -1 and ok(s + 3):
+                b_stage(s + 3, 1)
             if s == 0:
-                interleave(w_g[:], w_raw[:])
-            if 0 <= s - 1 < NP:
-                g2_stage(s - 1)
-            if 0 <= s - 2:
-                ml_stage(s - 2)
-            if 0 <= s - 1 < NP:
-                qn_stage(s - 1)
-            if s + 2 < NP:
+                interleave(nc.vector.tensor_copy, w_g[:], w_raw[:])
+            if ok(n1):
+                g2_stage(n1)
+            if ok(n2):
+                ml_stage(n2)
+            if ok(n1):
+                qn_stage(n1)
+            if s > -3 and ok(s + 2):
                 qa_stage(s + 2)
+            if s == -2:
+                nc.vector.quantize_mx(out=wo_codes[:].bitcast(FP8X4), scales=wo_scales[:], in_=wo_g[:].rearrange("p n j -> p (n j)"))
+                y_stage(0)
             if s == 0:
                 nc.vector.quantize_mx(out=w_codes[:].bitcast(FP8X4), scales=w_scales[:], in_=w_g[:].rearrange("p n j -> p (n j)"))
-            if 0 <= s - 1 < NP:
-                uv_stage(s - 1)
+            if ok(n1):
+                uv_stage(n1)

@@ -39,6 +39,8 @@ def tile_transformerblock_pb_t_kernel(tc, x, ao, wo_bytes, wo_scale, bo, g2, w1,
         nc.vector.memset(bo_row[:], 0.0)
         warm = const.tile([P, 1], F32)
         nc.vector.memset(warm[:], 0.0)
+        zeros = const.tile([P, D], BF16)
+        nc.vector.memset(zeros[:], 0.0)
         ones = const.tile([P, P], BF16)
         nc.vector.memset(ones[:], 1.0)
         neg_half = const.tile([P, 2], F32)
@@ -119,21 +121,26 @@ def tile_transformerblock_pb_t_kernel(tc, x, ao, wo_bytes, wo_scale, bo, g2, w1,
             codes, scales = st["qa", s]
             for a in range(2):
                 y = psum.tile([P, D], F32, name="y_ps")
-                nc.tensor.matmul_mx(
-                    out=y[:],
-                    lhsT=codes[:, a * P : (a + 1) * P].bitcast(FP8X4),
-                    lhsT_scale=scales[:, a * P : (a + 1) * P],
-                    rhs=wo_codes[:].bitcast(FP8X4),
-                    rhs_scale=wo_scales[:],
-                    start=True,
-                    stop=True,
-                )
+                for i in range(2):
+                    nc.tensor.matmul_mx(
+                        out=y[:],
+                        lhsT=codes[:, a * P : (a + 1) * P].bitcast(FP8X4),
+                        lhsT_scale=scales[:, a * P : (a + 1) * P],
+                        rhs=wo_codes[:].bitcast(FP8X4),
+                        rhs_scale=wo_scales[:],
+                        start=True,
+                        stop=True,
+                    )
                 st["y", s, a] = y
+
+        def on_vector(s, a):
+            return a == 1 and s % 2 == 1
 
         def b_stage(s, a):
             if a == 0:
                 st["x1", s] = res.tile([P, 2, D], F32, name="x1")
-            nc.gpsimd.tensor_tensor(out=st["x1", s][:, a, :], in0=x_t[2 * s + a], in1=bo_t[:], op=ALU.add)
+            eng = nc.vector if on_vector(s, a) else nc.gpsimd
+            eng.tensor_tensor(out=st["x1", s][:, a, :], in0=x_t[2 * s + a], in1=bo_t[:], op=ALU.add)
 
         def x_stage(s):
             x1 = st["x1", s]
@@ -228,6 +235,9 @@ def tile_transformerblock_pb_t_kernel(tc, x, ao, wo_bytes, wo_scale, bo, g2, w1,
         def interleave(copy, dst, src):
             copy(out=dst.rearrange("p (c i) t -> p c t i", i=4), in_=src.rearrange("p t (c i) -> p c t i", i=4))
 
+        warm_ps = psum1.tile([P, D], F32, name="v_ps")
+        for i in range(4):
+            nc.tensor.matmul(warm_ps[:], lhsT=ones[:], rhs=zeros[:], start=True, stop=True)
         bo_ps = psum1.tile([P, D], F32, name="u_ps")
         nc.tensor.matmul(bo_ps[:], lhsT=ones[:], rhs=bo_row[:], start=True, stop=True)
         nc.scalar.copy(out=bo_t[:], in_=bo_ps[:])
@@ -263,7 +273,7 @@ def tile_transformerblock_pb_t_kernel(tc, x, ao, wo_bytes, wo_scale, bo, g2, w1,
             if s >= 0 and ok(s + 1):
                 y_stage(s + 1)
             if ok(s + 3):
-                t_stage(s + 3)
+                t_stage(s + 3, 2 if s < 0 else 1)
             if s >= -1 and ok(s + 3):
                 b_stage(s + 3, 0)
             if ok(n0):

@@ -19,9 +19,12 @@ FLOPS = 2 * B * S * (H * DK * D + D * 2 * F)
 P = 128
 J = 4
 I = S // P
-PAIRS_B = I // 2
-NP = B * PAIRS_B
-CHUNKS = ((0, 0, 2), (0, 2, 2), (0, 4, 4), (0, 8, 8), (1, 0, 8), (1, 8, 8))
+TILES = B * I
+WIDTHS = (1, 1) + (2,) * 14 + (1, 1)
+NU = len(WIDTHS)
+FIRST = tuple(sum(WIDTHS[:u]) for u in range(NU))
+CUT = 320
+C = D // P
 
 
 def tile_transformerblock_pb_t_kernel(tc, x, ao, wo_bytes, wo_scale, bo, g2, w1, w3, out_0, out_1):
@@ -29,30 +32,34 @@ def tile_transformerblock_pb_t_kernel(tc, x, ao, wo_bytes, wo_scale, bo, g2, w1,
     with ExitStack() as ctx:
         const = ctx.enter_context(tc.tile_pool(name="const", bufs=1))
         loads = ctx.enter_context(tc.tile_pool(name="loads", bufs=1))
-        res = ctx.enter_context(tc.tile_pool(name="res", bufs=NP))
+        res = ctx.enter_context(tc.tile_pool(name="res", bufs=NU))
+        hres = ctx.enter_context(tc.tile_pool(name="hres", bufs=10))
         work = ctx.enter_context(tc.tile_pool(name="work", bufs=3))
         psum = ctx.enter_context(tc.psum_pool(name="psum", bufs=2))
         psum1 = ctx.enter_context(tc.psum_pool(name="psum1", bufs=1))
         ctx.enter_context(tc.manual_schedule())
 
-        bo_row = const.tile([P, D], BF16)
-        nc.vector.memset(bo_row[:], 0.0)
-        warm = const.tile([P, 1], F32)
-        nc.vector.memset(warm[:], 0.0)
-        zeros = const.tile([P, D], BF16)
-        nc.vector.memset(zeros[:], 0.0)
+        bo_rows = const.tile([P, P], BF16)
+        nc.vector.memset(bo_rows[:], 0.0)
+        g2_row = const.tile([P, D], BF16)
+        nc.vector.memset(g2_row[:], 0.0)
         ones = const.tile([P, P], BF16)
         nc.vector.memset(ones[:], 1.0)
+        zeros = const.tile([P, D], BF16)
+        nc.vector.memset(zeros[:], 0.0)
+        warm = const.tile([P, 1], F32)
+        nc.vector.memset(warm[:], 0.0)
         neg_half = const.tile([P, 2], F32)
         nc.gpsimd.memset(neg_half[:], -0.5)
         ident = const.tile([P, P], F32)
         make_identity(nc, ident[:])
+        ident_bf = const.tile([P, P], BF16)
+        nc.vector.tensor_copy(out=ident_bf[:], in_=ident[:])
 
         wsc = const.tile([P, J], F32)
         nc.scalar.dma_start(out=wsc[:], in_=wo_scale.rearrange("(p t) o -> p (t o)", t=J))
-        nc.scalar.dma_start(out=bo_row[0:1, :], in_=bo.rearrange("(o n) -> o n", o=1))
-        g2t = const.tile([P, J], BF16)
-        nc.scalar.dma_start(out=g2t[:], in_=g2.rearrange("(p t) -> p t", t=J))
+        nc.scalar.dma_start(out=bo_rows[0:C, :], in_=bo.rearrange("(c p) -> c p", c=C))
+        nc.scalar.dma_start(out=g2_row[0:1, :], in_=g2.rearrange("(o n) -> o n", o=1))
         warm2 = const.tile([P, 1], F32)
         nc.scalar.activation(out=warm2[:], in_=warm[:], func=ACT.Silu)
 
@@ -61,146 +68,160 @@ def tile_transformerblock_pb_t_kernel(tc, x, ao, wo_bytes, wo_scale, bo, g2, w1,
         ao_t = {}
         x_t = {}
 
-        def load_ao(c):
-            b, i0, n = CHUNKS[c]
-            t = loads.tile([P, n, H, DK], BF16, name="ao%d" % c, align_bytes=64)
+        def load(k0, n):
+            b, i0 = k0 // I, k0 % I
             src = ao[b].rearrange("h (p i) d -> p i h d", i=I)
             for i in range(n):
-                nc.sync.dma_start(out=t[:, i, :, :], in_=src[:, i0 + i, :, :])
-                ao_t[b * I + i0 + i] = t[:, i, :, :]
-
-        def load_x(c):
-            b, i0, n = CHUNKS[c]
-            t = loads.tile([P, n, D], BF16, name="x%d" % c, align_bytes=64)
-            nc.sync.dma_start(out=t[:], in_=x[b].rearrange("(p i) d -> p i d", i=I)[:, i0 : i0 + n, :])
+                at = loads.tile([P, H, DK], BF16, name="ao%d" % (k0 + i), align_bytes=64)
+                nc.sync.dma_start(out=at[:], in_=src[:, i0 + i, :, :])
+                ao_t[k0 + i] = at
+            xt = loads.tile([P, n, D], BF16, name="x%d" % k0, align_bytes=64)
+            nc.sync.dma_start(out=xt[:], in_=x[b].rearrange("(p i) d -> p i d", i=I)[:, i0 : i0 + n, :])
             for i in range(n):
-                x_t[b * I + i0 + i] = t[:, i, :]
+                x_t[k0 + i] = xt[:, i, :]
 
-        load_ao(0)
-        load_x(0)
-        w_raw = const.tile([P, J, 2 * F], BF16, align_bytes=64)
-        load_ao(1)
-        nc.sync.dma_start(out=w_raw[:, :, 0:F], in_=w1.rearrange("(p j) f -> p j f", j=J))
-        nc.sync.dma_start(out=w_raw[:, :, F : 2 * F], in_=w3.rearrange("(p j) f -> p j f", j=J))
-        load_x(1)
-        for c in range(2, len(CHUNKS)):
-            load_ao(c)
-            load_x(c)
+        w_raw1 = const.tile([P, J, F], BF16, align_bytes=64)
+        w_raw3 = const.tile([P, J, F], BF16, align_bytes=64)
+        load(0, 1)
+        load(1, 1)
+        load(2, 2)
+        nc.sync.dma_start(out=w_raw1[:], in_=w1.rearrange("(p j) f -> p j f", j=J))
+        nc.sync.dma_start(out=w_raw3[:], in_=w3.rearrange("(p j) f -> p j f", j=J))
+        for k0 in range(4, TILES, 4):
+            load(k0, 4)
 
         st = {}
 
-        def t_stage(s, dummies=1):
-            bank = psum.tile([P, 2, 2, P], F32, name="aT_ps")
+        def span(u):
+            return range(WIDTHS[u])
+
+        def hbm_rows(t, u, width):
+            b, i0 = FIRST[u] // I, FIRST[u] % I
+            return t[b].rearrange("(p i) d -> p i d", i=I)[:, i0 : i0 + WIDTHS[u], :]
+
+        def t_stage(u, dummies=0):
+            bank = psum1.tile([P, 2, 2, P], F32, name="aT_ps")
             for i in range(dummies):
-                nc.tensor.matmul(bank[:].rearrange("p a u r -> p (a u r)"), lhsT=ones[:], rhs=bo_row[:], start=True, stop=True)
-            for a in range(2):
-                words = ao_t[2 * s + a].rearrange("p h d -> p (h d)").bitcast(F32)
-                for u in range(2):
-                    nc.tensor.transpose(bank[:, a, u, :], words[:, u : 2 * P : 2], ident[:])
-            st["aT", s] = bank
+                nc.tensor.matmul(bank[:].rearrange("p a u r -> p (a u r)"), lhsT=ones[:], rhs=zeros[:], start=True, stop=True)
+            for a in span(u):
+                words = ao_t[FIRST[u] + a][:].rearrange("p h d -> p (h d)").bitcast(F32)
+                for e in range(2):
+                    nc.tensor.transpose(bank[:, a, e, :], words[:, e : 2 * P : 2], ident[:])
+            st["aT", u] = bank
 
-        def c_stage(s):
-            bank = st["aT", s]
-            g = work.tile([P, 2, P, J], BF16, name="ag", align_bytes=64)
-            nc.scalar.copy(
-                out=g[:].rearrange("p a r j -> p (a r j)").bitcast(F32).rearrange("p (a r u) -> p a r u", a=2, u=2),
-                in_=bank[:].rearrange("p a u r -> p a r u"),
+        def copy_words(copy, bank, u, name):
+            n = WIDTHS[u]
+            g = work.tile([P, 2, P, J], BF16, name=name, align_bytes=64)
+            copy(
+                out=g[:, 0:n].rearrange("p a r j -> p (a r j)").bitcast(F32).rearrange("p (a r e) -> p a r e", a=n, e=2),
+                in_=bank[:, 0:n].rearrange("p a e r -> p a r e"),
             )
-            st["ag", s] = g
+            return g
 
-        def quant(src, name):
+        def c_stage(u):
+            st["ag", u] = copy_words(nc.scalar.copy, st["aT", u], u, "ag")
+
+        def quant(u, src, name):
+            n = WIDTHS[u]
             codes = work.tile([P, 2 * P], U32, name=name + "c", align_bytes=64)
             scales = work.tile([P, 2 * P], U8, name=name + "s", align_bytes=64)
-            nc.vector.quantize_mx(out=codes[:].bitcast(FP8X4), scales=scales[:], in_=src[:].rearrange("p a r j -> p (a r j)"))
+            nc.vector.quantize_mx(
+                out=codes[:, 0 : n * P].bitcast(FP8X4), scales=scales[:, 0 : n * P], in_=src[:, 0:n].rearrange("p a r j -> p (a r j)")
+            )
             return codes, scales
 
-        def qa_stage(s):
-            st["qa", s] = quant(st["ag", s], "qa")
+        def qa_stage(u):
+            st["qa", u] = quant(u, st["ag", u], "qa")
 
-        def y_stage(s):
-            codes, scales = st["qa", s]
-            for a in range(2):
-                y = psum.tile([P, D], F32, name="y_ps")
-                for i in range(2):
-                    nc.tensor.matmul_mx(
-                        out=y[:],
-                        lhsT=codes[:, a * P : (a + 1) * P].bitcast(FP8X4),
-                        lhsT_scale=scales[:, a * P : (a + 1) * P],
-                        rhs=wo_codes[:].bitcast(FP8X4),
-                        rhs_scale=wo_scales[:],
-                        start=True,
-                        stop=True,
-                    )
-                st["y", s, a] = y
+        def yt_stage(u):
+            codes, scales = st["qa", u]
+            cols = slice(0, WIDTHS[u] * P)
+            for c in range(C):
+                if c % 2 == 0:
+                    bank = psum.tile([P, 2, 2 * P], F32, name="yT_ps")
+                    st["yT", u, c // 2] = bank
+                nc.tensor.matmul_mx(
+                    out=bank[:, c % 2, cols],
+                    lhsT=wo_codes[:, c * P : (c + 1) * P].bitcast(FP8X4),
+                    lhsT_scale=wo_scales[:, c * P : (c + 1) * P],
+                    rhs=codes[:, cols].bitcast(FP8X4),
+                    rhs_scale=scales[:, cols],
+                    start=True,
+                    stop=True,
+                )
 
-        def on_vector(s, a):
-            return a == 1 and s % 2 == 1
+        def yb_stage(u):
+            cols = slice(0, WIDTHS[u] * P)
+            yb = st["yb", u]
+            for c in range(C - 1):
+                nc.scalar.activation(out=yb[:, c, cols], in_=st["yT", u, c // 2][:, c % 2, cols], func=ACT.Identity, bias=bo_col[:, c : c + 1])
 
-        def b_stage(s, a):
-            if a == 0:
-                st["x1", s] = res.tile([P, 2, D], F32, name="x1")
-            eng = nc.vector if on_vector(s, a) else nc.gpsimd
-            eng.tensor_tensor(out=st["x1", s][:, a, :], in0=x_t[2 * s + a], in1=bo_t[:], op=ALU.add)
+        def ybv_stage(u):
+            cols = slice(0, WIDTHS[u] * P)
+            st["yb", u] = work.tile([P, C, 2 * P], F32, name="yb")
+            nc.vector.tensor_scalar(
+                out=st["yb", u][:, 3, cols], in0=st["yT", u, 1][:, 1, cols], scalar1=bo_col[:, 3:4], scalar2=None, op0=ALU.add
+            )
 
-        def x_stage(s):
-            x1 = st["x1", s]
-            for a in range(2):
-                nc.vector.tensor_tensor(out=x1[:, a, :], in0=st["y", s, a][:], in1=x1[:, a, :], op=ALU.add)
-            b, i0 = s // PAIRS_B, 2 * (s % PAIRS_B)
-            nc.sync.dma_start(out=out_0[b].rearrange("(p i) d -> p i d", i=I)[:, i0 : i0 + 2, :], in_=x1[:])
+        def yk_stage(u):
+            for a in span(u):
+                bank = psum.tile([P, C, P], F32, name="y_ps")
+                if a == 0:
+                    nc.tensor.matmul(bank[:].rearrange("p c q -> p (c q)"), lhsT=ones[:], rhs=zeros[:], start=True, stop=True)
+                for c in range(C):
+                    nc.tensor.transpose(bank[:, c, :], st["yb", u][:, c, a * P : (a + 1) * P], ident[:])
+                st["y", u, a] = bank
 
-        def sq_stage(s):
+        def x_stage(u):
+            x1 = res.tile([P, 2, D], F32, name="x1")
+            for a in span(u):
+                nc.vector.tensor_tensor(out=x1[:, a, :], in0=st["y", u, a][:].rearrange("p c q -> p (c q)"), in1=x_t[FIRST[u] + a], op=ALU.add)
+            st["x1", u] = x1
+            nc.sync.dma_start(out=hbm_rows(out_0, u, D), in_=x1[:, 0 : WIDTHS[u], :])
+
+        def sq_stage(u):
             ssum = work.tile([P, 2], F32, name="ssum")
-            for a in range(2):
+            for a in span(u):
                 junk = work.tile([P, D], BF16, name="junk")
-                nc.scalar.activation(out=junk[:], in_=st["x1", s][:, a, :], func=ACT.Square, accum_out=ssum[:, a : a + 1])
-            st["ssum", s] = ssum
+                nc.scalar.activation(out=junk[:], in_=st["x1", u][:, a, :], func=ACT.Square, accum_out=ssum[:, a : a + 1])
+            st["ssum", u] = ssum
 
-        def r_stage(s):
+        def r_stage(u):
+            n = WIDTHS[u]
             ms = work.tile([P, 2], F32, name="ms")
-            nc.gpsimd.tensor_scalar(out=ms[:], in0=st["ssum", s][:], scalar1=1.0 / D, scalar2=EPS, op0=ALU.mult, op1=ALU.add)
+            nc.vector.tensor_scalar(out=ms[:, 0:n], in0=st["ssum", u][:, 0:n], scalar1=1.0 / D, scalar2=EPS, op0=ALU.mult, op1=ALU.add)
             rstd = work.tile([P, 2], F32, name="rstd")
-            nc.gpsimd.tensor_tensor(out=rstd[:], in0=ms[:], in1=neg_half[:], op=ALU.pow)
-            st["rstd", s] = rstd
+            nc.gpsimd.tensor_tensor(out=rstd[:, 0:n], in0=ms[:, 0:n], in1=neg_half[:, 0:n], op=ALU.pow)
+            st["rstd", u] = rstd
 
-        def n_stage(s):
-            for a in range(2):
-                xn = work.tile([P, J, P], F32, name="xn%d" % a)
-                nc.scalar.activation(
-                    out=xn[:].rearrange("p t q -> p q t"),
-                    in_=st["x1", s][:, a, :].rearrange("p (q t) -> p q t", t=J),
-                    func=ACT.Copy,
-                    scale=st["rstd", s][:, a : a + 1],
+        def n_stage(u):
+            for a in span(u):
+                xn = work.tile([P, D], BF16, name="xn%d" % a, align_bytes=64)
+                nc.vector.scalar_tensor_tensor(
+                    out=xn[:], in0=st["x1", u][:, a, :], scalar=st["rstd", u][:, a : a + 1], in1=g2_all[:], op0=ALU.mult, op1=ALU.mult
                 )
-                st["xn", s, a] = xn
+                st["xn", u, a] = xn
 
-        def nt_stage(s):
-            for a in range(2):
-                bank = psum.tile([P, J, P], F32, name="nT_ps")
-                for t in range(J):
-                    nc.tensor.transpose(bank[:, t, :], st["xn", s, a][:, t, :], ident[:])
-                st["nT", s, a] = bank
+        def nt_stage(u):
+            bank = psum1.tile([P, 2, 2, P], F32, name="nT_ps")
+            for a in span(u):
+                words = st["xn", u, a][:].bitcast(F32)
+                for e in range(2):
+                    nc.tensor.transpose(bank[:, a, e, :], words[:, e : 2 * P : 2], ident[:])
+            st["nT", u] = bank
 
-        def g2_stage(s):
-            ng = work.tile([P, 2, P, J], BF16, name="ng", align_bytes=64)
-            for a in range(2):
-                nc.vector.tensor_tensor(
-                    out=ng[:, a, :, :],
-                    in0=st["nT", s, a][:].rearrange("p t r -> p r t"),
-                    in1=g2t[:].unsqueeze(1).to_broadcast([P, P, J]),
-                    op=ALU.mult,
-                )
-            st["ng", s] = ng
+        def nc_stage(u):
+            st["ng", u] = copy_words(nc.scalar.copy, st["nT", u], u, "ng")
 
-        def qn_stage(s):
-            st["qn", s] = quant(st["ng", s], "qn")
+        def qn_stage(u):
+            st["qn", u] = quant(u, st["ng", u], "qn")
 
-        def uv_stage(s):
-            codes, scales = st["qn", s]
-            u = psum1.tile([P, 2, F], F32, name="u_ps")
-            v = psum1.tile([P, 2, F], F32, name="v_ps")
-            for a in range(2):
-                for dst, f0 in ((u, 0), (v, F)):
+        def uv_stage(u):
+            codes, scales = st["qn", u]
+            gate = psum1.tile([P, 2, F], F32, name="u_ps")
+            up = psum1.tile([P, 2, F], F32, name="v_ps")
+            for a in span(u):
+                for dst, f0 in ((gate, 0), (up, F)):
                     nc.tensor.matmul_mx(
                         out=dst[:, a, :],
                         lhsT=codes[:, a * P : (a + 1) * P].bitcast(FP8X4),
@@ -210,18 +231,19 @@ def tile_transformerblock_pb_t_kernel(tc, x, ao, wo_bytes, wo_scale, bo, g2, w1,
                         start=True,
                         stop=True,
                     )
-            st["uv", s] = (u, v)
+            st["uv", u] = (gate, up)
 
-        def sl_stage(s):
+        def sl_stage(u):
+            n = WIDTHS[u]
             sil = work.tile([P, 2, F], F32, name="sil")
-            nc.scalar.activation(out=sil[:], in_=st["uv", s][0][:], func=ACT.Silu)
-            st["sil", s] = sil
+            nc.scalar.activation(out=sil[:, 0:n], in_=st["uv", u][0][:, 0:n], func=ACT.Silu)
+            st["sil", u] = sil
 
-        def ml_stage(s):
-            h = work.tile([P, 2, F], F32, name="h")
-            nc.vector.tensor_tensor(out=h[:], in0=st["uv", s][1][:], in1=st["sil", s][:], op=ALU.mult)
-            b, i0 = s // PAIRS_B, 2 * (s % PAIRS_B)
-            nc.sync.dma_start(out=out_1[b].rearrange("(p i) f -> p i f", i=I)[:, i0 : i0 + 2, :], in_=h[:])
+        def ml_stage(u):
+            n = WIDTHS[u]
+            h = hres.tile([P, 2, F], F32, name="h")
+            nc.vector.tensor_tensor(out=h[:, 0:n], in0=st["uv", u][1][:, 0:n], in1=st["sil", u][:, 0:n], op=ALU.mult)
+            nc.sync.dma_start(out=hbm_rows(out_1, u, F), in_=h[:, 0:n, :])
 
         wide = const.tile([P, J, D], BF16, align_bytes=64)
         wo_g = const.tile([P, D, J], BF16, align_bytes=64)
@@ -230,7 +252,8 @@ def tile_transformerblock_pb_t_kernel(tc, x, ao, wo_bytes, wo_scale, bo, g2, w1,
         w_g = const.tile([P, 2 * F, J], BF16, align_bytes=64)
         w_codes = const.tile([P, 2 * F], U32, align_bytes=64)
         w_scales = const.tile([P, 2 * F], U8, align_bytes=64)
-        bo_t = const.tile([P, D], BF16)
+        bo_col = const.tile([P, C], F32)
+        g2_all = const.tile([P, D], BF16)
 
         def interleave(copy, dst, src):
             copy(out=dst.rearrange("p (c i) t -> p c t i", i=4), in_=src.rearrange("p t (c i) -> p c t i", i=4))
@@ -238,62 +261,61 @@ def tile_transformerblock_pb_t_kernel(tc, x, ao, wo_bytes, wo_scale, bo, g2, w1,
         warm_ps = psum1.tile([P, D], F32, name="v_ps")
         for i in range(4):
             nc.tensor.matmul(warm_ps[:], lhsT=ones[:], rhs=zeros[:], start=True, stop=True)
-        bo_ps = psum1.tile([P, D], F32, name="u_ps")
-        nc.tensor.matmul(bo_ps[:], lhsT=ones[:], rhs=bo_row[:], start=True, stop=True)
-        nc.scalar.copy(out=bo_t[:], in_=bo_ps[:])
         for t in range(J):
             if t < 3:
                 nc.vector.tensor_scalar(out=wide[:, t, :], in0=wob[:, t, :].bitcast(FP8), scalar1=wsc[:, t : t + 1], scalar2=None, op0=ALU.mult)
             else:
                 nc.scalar.activation(out=wide[:, t, :], in_=wob[:, t, :].bitcast(FP8), func=ACT.Copy, scale=wsc[:, t : t + 1])
 
-        CUT = 320
-        for s in range(-3, NP + 3):
-            n0, n1, n2 = s - 1, s - 2, s - 3
+        def ok(u):
+            return 0 <= u < NU
 
-            def ok(i):
-                return 0 <= i < NP
-
-            if ok(n1):
-                nt_stage(n1)
-            if ok(n2):
-                sl_stage(n2)
+        for s in range(-3, NU + 4):
+            if ok(s - 2):
+                nt_stage(s - 2)
+            if ok(s + 3):
+                t_stage(s + 3)
+            if ok(s - 3):
+                sl_stage(s - 3)
+            if ok(s - 2):
+                nc_stage(s - 2)
+            if ok(s + 2):
+                qa_stage(s + 2)
+            if ok(s - 1):
+                r_stage(s - 1)
             if ok(s):
                 x_stage(s)
                 sq_stage(s)
-                r_stage(s)
-            if s > -3 and ok(s + 2):
-                c_stage(s + 2)
-            if s == -2:
+            if s == -3:
                 interleave(nc.vector.tensor_copy, wo_g[:, 0:CUT, :], wide[:, :, 0:CUT])
                 interleave(nc.scalar.copy, wo_g[:, CUT:D, :], wide[:, :, CUT:D])
-                for i in range(2):
-                    b_stage(i, 0)
-                    b_stage(i, 1)
-            if s >= 0 and ok(s + 1):
-                y_stage(s + 1)
-            if ok(s + 3):
-                t_stage(s + 3, 2 if s < 0 else 1)
-            if s >= -1 and ok(s + 3):
-                b_stage(s + 3, 0)
-            if ok(n0):
-                n_stage(n0)
-            if s >= -1 and ok(s + 3):
-                b_stage(s + 3, 1)
-            if s == 0:
-                interleave(nc.vector.tensor_copy, w_g[:], w_raw[:])
-            if ok(n1):
-                g2_stage(n1)
-            if ok(n2):
-                ml_stage(n2)
-            if ok(n1):
-                qn_stage(n1)
-            if s > -3 and ok(s + 2):
-                qa_stage(s + 2)
-            if s == -2:
                 nc.vector.quantize_mx(out=wo_codes[:].bitcast(FP8X4), scales=wo_scales[:], in_=wo_g[:].rearrange("p n j -> p (n j)"))
-                y_stage(0)
+                bo_ps = psum1.tile([P, P], F32, name="nT_ps")
+                nc.tensor.matmul(bo_ps[:], lhsT=bo_rows[:], rhs=ident_bf[:], start=True, stop=True)
+                nc.scalar.copy(out=bo_col[:], in_=bo_ps[:, 0:C])
+            if ok(s + 2):
+                yt_stage(s + 2)
+            if ok(s + 3):
+                c_stage(s + 3)
+            if s == -1:
+                g2_ps = psum1.tile([P, D], F32, name="u_ps")
+                nc.tensor.matmul(g2_ps[:], lhsT=ones[:], rhs=g2_row[:], start=True, stop=True)
+                nc.scalar.copy(out=g2_all[:], in_=g2_ps[:])
+            if ok(s + 1):
+                yk_stage(s + 1)
             if s == 0:
+                interleave(nc.vector.tensor_copy, w_g[:, 0:F, :], w_raw1[:])
+                interleave(nc.vector.tensor_copy, w_g[:, F : 2 * F, :], w_raw3[:])
+            if ok(s - 3):
+                ml_stage(s - 3)
+            if ok(s + 2):
+                ybv_stage(s + 2)
+                yb_stage(s + 2)
+            if ok(s - 2):
+                qn_stage(s - 2)
+            if s == 1:
                 nc.vector.quantize_mx(out=w_codes[:].bitcast(FP8X4), scales=w_scales[:], in_=w_g[:].rearrange("p n j -> p (n j)"))
-            if ok(n1):
-                uv_stage(n1)
+            if ok(s - 1):
+                n_stage(s - 1)
+            if ok(s - 2):
+                uv_stage(s - 2)

from contextlib import ExitStack

import concourse.mybir as mybir
from concourse.masks import make_identity

F32 = mybir.dt.float32
BF16 = mybir.dt.bfloat16
U32 = mybir.dt.uint32
U8 = mybir.dt.uint8
FP8 = mybir.dt.float8_e4m3fn
FP8X4 = mybir.dt.float8_e4m3fn_x4
ACT = mybir.ActivationFunctionType
ALU = mybir.AluOpType

B, S, D, H, DK, F = 2, 2048, 512, 4, 128, 256
EPS = 1e-6
FLOPS = 2 * B * S * (H * DK * D + D * 2 * F)

P = 128
J = 4
I = S // P
TILES = B * I
WIDTHS = (1, 1) + (2,) * 14 + (1, 1)
NU = len(WIDTHS)
FIRST = tuple(sum(WIDTHS[:u]) for u in range(NU))
CUT = 320
C = D // P


def tile_transformerblock_pb_t_kernel(tc, x, ao, wo_bytes, wo_scale, bo, g2, w1, w3, out_0, out_1):
    nc = tc.nc
    with ExitStack() as ctx:
        const = ctx.enter_context(tc.tile_pool(name="const", bufs=1))
        loads = ctx.enter_context(tc.tile_pool(name="loads", bufs=1))
        res = ctx.enter_context(tc.tile_pool(name="res", bufs=NU))
        hres = ctx.enter_context(tc.tile_pool(name="hres", bufs=10))
        work = ctx.enter_context(tc.tile_pool(name="work", bufs=3))
        psum = ctx.enter_context(tc.psum_pool(name="psum", bufs=2))
        psum1 = ctx.enter_context(tc.psum_pool(name="psum1", bufs=1))
        ctx.enter_context(tc.manual_schedule())

        bo_rows = const.tile([P, P], BF16)
        nc.vector.memset(bo_rows[:], 0.0)
        g2_row = const.tile([P, D], BF16)
        nc.vector.memset(g2_row[:], 0.0)
        ones = const.tile([P, P], BF16)
        nc.vector.memset(ones[:], 1.0)
        zeros = const.tile([P, D], BF16)
        nc.vector.memset(zeros[:], 0.0)
        warm = const.tile([P, 1], F32)
        nc.vector.memset(warm[:], 0.0)
        neg_half = const.tile([P, 2], F32)
        nc.gpsimd.memset(neg_half[:], -0.5)
        ident = const.tile([P, P], F32)
        make_identity(nc, ident[:])
        ident_bf = const.tile([P, P], BF16)
        nc.vector.tensor_copy(out=ident_bf[:], in_=ident[:])

        wsc = const.tile([P, J], F32)
        nc.scalar.dma_start(out=wsc[:], in_=wo_scale.rearrange("(p t) o -> p (t o)", t=J))
        nc.scalar.dma_start(out=bo_rows[0:C, :], in_=bo.rearrange("(c p) -> c p", c=C))
        nc.scalar.dma_start(out=g2_row[0:1, :], in_=g2.rearrange("(o n) -> o n", o=1))
        warm2 = const.tile([P, 1], F32)
        nc.scalar.activation(out=warm2[:], in_=warm[:], func=ACT.Silu)

        wob = const.tile([P, J, D], U8, align_bytes=64)
        nc.sync.dma_start(out=wob[:], in_=wo_bytes.rearrange("(p t) n -> p t n", t=J))
        ao_t = {}
        x_t = {}

        def load(k0, n):
            b, i0 = k0 // I, k0 % I
            src = ao[b].rearrange("h (p i) d -> p i h d", i=I)
            for i in range(n):
                at = loads.tile([P, H, DK], BF16, name="ao%d" % (k0 + i), align_bytes=64)
                nc.sync.dma_start(out=at[:], in_=src[:, i0 + i, :, :])
                ao_t[k0 + i] = at
            xt = loads.tile([P, n, D], BF16, name="x%d" % k0, align_bytes=64)
            nc.sync.dma_start(out=xt[:], in_=x[b].rearrange("(p i) d -> p i d", i=I)[:, i0 : i0 + n, :])
            for i in range(n):
                x_t[k0 + i] = xt[:, i, :]

        w_raw1 = const.tile([P, J, F], BF16, align_bytes=64)
        w_raw3 = const.tile([P, J, F], BF16, align_bytes=64)
        load(0, 1)
        load(1, 1)
        load(2, 2)
        nc.sync.dma_start(out=w_raw1[:], in_=w1.rearrange("(p j) f -> p j f", j=J))
        nc.sync.dma_start(out=w_raw3[:], in_=w3.rearrange("(p j) f -> p j f", j=J))
        for k0 in range(4, TILES, 4):
            load(k0, 4)

        st = {}

        def span(u):
            return range(WIDTHS[u])

        def hbm_rows(t, u, width):
            b, i0 = FIRST[u] // I, FIRST[u] % I
            return t[b].rearrange("(p i) d -> p i d", i=I)[:, i0 : i0 + WIDTHS[u], :]

        def t_stage(u, dummies=0):
            bank = psum1.tile([P, 2, 2, P], F32, name="aT_ps")
            for i in range(dummies):
                nc.tensor.matmul(bank[:].rearrange("p a u r -> p (a u r)"), lhsT=ones[:], rhs=zeros[:], start=True, stop=True)
            for a in span(u):
                words = ao_t[FIRST[u] + a][:].rearrange("p h d -> p (h d)").bitcast(F32)
                for e in range(2):
                    nc.tensor.transpose(bank[:, a, e, :], words[:, e : 2 * P : 2], ident[:])
            st["aT", u] = bank

        def copy_words(copy, bank, u, name):
            n = WIDTHS[u]
            g = work.tile([P, 2, P, J], BF16, name=name, align_bytes=64)
            copy(
                out=g[:, 0:n].rearrange("p a r j -> p (a r j)").bitcast(F32).rearrange("p (a r e) -> p a r e", a=n, e=2),
                in_=bank[:, 0:n].rearrange("p a e r -> p a r e"),
            )
            return g

        def c_stage(u):
            st["ag", u] = copy_words(nc.scalar.copy, st["aT", u], u, "ag")

        def quant(u, src, name):
            n = WIDTHS[u]
            codes = work.tile([P, 2 * P], U32, name=name + "c", align_bytes=64)
            scales = work.tile([P, 2 * P], U8, name=name + "s", align_bytes=64)
            nc.vector.quantize_mx(
                out=codes[:, 0 : n * P].bitcast(FP8X4), scales=scales[:, 0 : n * P], in_=src[:, 0:n].rearrange("p a r j -> p (a r j)")
            )
            return codes, scales

        def qa_stage(u):
            st["qa", u] = quant(u, st["ag", u], "qa")

        def yt_stage(u):
            codes, scales = st["qa", u]
            cols = slice(0, WIDTHS[u] * P)
            for c in range(C):
                if c % 2 == 0:
                    bank = psum.tile([P, 2, 2 * P], F32, name="yT_ps")
                    st["yT", u, c // 2] = bank
                nc.tensor.matmul_mx(
                    out=bank[:, c % 2, cols],
                    lhsT=wo_codes[:, c * P : (c + 1) * P].bitcast(FP8X4),
                    lhsT_scale=wo_scales[:, c * P : (c + 1) * P],
                    rhs=codes[:, cols].bitcast(FP8X4),
                    rhs_scale=scales[:, cols],
                    start=True,
                    stop=True,
                )

        def yb_stage(u):
            cols = slice(0, WIDTHS[u] * P)
            yb = st["yb", u]
            for c in range(C - 1):
                nc.scalar.activation(out=yb[:, c, cols], in_=st["yT", u, c // 2][:, c % 2, cols], func=ACT.Identity, bias=bo_col[:, c : c + 1])

        def ybv_stage(u):
            cols = slice(0, WIDTHS[u] * P)
            st["yb", u] = work.tile([P, C, 2 * P], F32, name="yb")
            nc.vector.tensor_scalar(
                out=st["yb", u][:, 3, cols], in0=st["yT", u, 1][:, 1, cols], scalar1=bo_col[:, 3:4], scalar2=None, op0=ALU.add
            )

        def yk_stage(u):
            for a in span(u):
                bank = psum.tile([P, C, P], F32, name="y_ps")
                if a == 0:
                    nc.tensor.matmul(bank[:].rearrange("p c q -> p (c q)"), lhsT=ones[:], rhs=zeros[:], start=True, stop=True)
                for c in range(C):
                    nc.tensor.transpose(bank[:, c, :], st["yb", u][:, c, a * P : (a + 1) * P], ident[:])
                st["y", u, a] = bank

        def x_stage(u):
            x1 = res.tile([P, 2, D], F32, name="x1")
            for a in span(u):
                nc.vector.tensor_tensor(out=x1[:, a, :], in0=st["y", u, a][:].rearrange("p c q -> p (c q)"), in1=x_t[FIRST[u] + a], op=ALU.add)
            st["x1", u] = x1
            nc.sync.dma_start(out=hbm_rows(out_0, u, D), in_=x1[:, 0 : WIDTHS[u], :])

        def sq_stage(u):
            ssum = work.tile([P, 2], F32, name="ssum")
            for a in span(u):
                junk = work.tile([P, D], BF16, name="junk")
                nc.scalar.activation(out=junk[:], in_=st["x1", u][:, a, :], func=ACT.Square, accum_out=ssum[:, a : a + 1])
            st["ssum", u] = ssum

        def r_stage(u):
            n = WIDTHS[u]
            ms = work.tile([P, 2], F32, name="ms")
            nc.vector.tensor_scalar(out=ms[:, 0:n], in0=st["ssum", u][:, 0:n], scalar1=1.0 / D, scalar2=EPS, op0=ALU.mult, op1=ALU.add)
            rstd = work.tile([P, 2], F32, name="rstd")
            nc.gpsimd.tensor_tensor(out=rstd[:, 0:n], in0=ms[:, 0:n], in1=neg_half[:, 0:n], op=ALU.pow)
            st["rstd", u] = rstd

        def n_stage(u):
            for a in span(u):
                xn = work.tile([P, D], BF16, name="xn%d" % a, align_bytes=64)
                nc.vector.scalar_tensor_tensor(
                    out=xn[:], in0=st["x1", u][:, a, :], scalar=st["rstd", u][:, a : a + 1], in1=g2_all[:], op0=ALU.mult, op1=ALU.mult
                )
                st["xn", u, a] = xn

        def nt_stage(u):
            bank = psum1.tile([P, 2, 2, P], F32, name="nT_ps")
            for a in span(u):
                words = st["xn", u, a][:].bitcast(F32)
                for e in range(2):
                    nc.tensor.transpose(bank[:, a, e, :], words[:, e : 2 * P : 2], ident[:])
            st["nT", u] = bank

        def nc_stage(u):
            st["ng", u] = copy_words(nc.scalar.copy, st["nT", u], u, "ng")

        def qn_stage(u):
            st["qn", u] = quant(u, st["ng", u], "qn")

        def uv_stage(u):
            codes, scales = st["qn", u]
            gate = psum1.tile([P, 2, F], F32, name="u_ps")
            up = psum1.tile([P, 2, F], F32, name="v_ps")
            for a in span(u):
                for dst, f0 in ((gate, 0), (up, F)):
                    nc.tensor.matmul_mx(
                        out=dst[:, a, :],
                        lhsT=codes[:, a * P : (a + 1) * P].bitcast(FP8X4),
                        lhsT_scale=scales[:, a * P : (a + 1) * P],
                        rhs=w_codes[:, f0 : f0 + F].bitcast(FP8X4),
                        rhs_scale=w_scales[:, f0 : f0 + F],
                        start=True,
                        stop=True,
                    )
            st["uv", u] = (gate, up)

        def sl_stage(u):
            n = WIDTHS[u]
            sil = work.tile([P, 2, F], F32, name="sil")
            nc.scalar.activation(out=sil[:, 0:n], in_=st["uv", u][0][:, 0:n], func=ACT.Silu)
            st["sil", u] = sil

        def ml_stage(u):
            n = WIDTHS[u]
            h = hres.tile([P, 2, F], F32, name="h")
            nc.vector.tensor_tensor(out=h[:, 0:n], in0=st["uv", u][1][:, 0:n], in1=st["sil", u][:, 0:n], op=ALU.mult)
            nc.sync.dma_start(out=hbm_rows(out_1, u, F), in_=h[:, 0:n, :])

        wide = const.tile([P, J, D], BF16, align_bytes=64)
        wo_g = const.tile([P, D, J], BF16, align_bytes=64)
        wo_codes = const.tile([P, D], U32, align_bytes=64)
        wo_scales = const.tile([P, D], U8, align_bytes=64)
        w_g = const.tile([P, 2 * F, J], BF16, align_bytes=64)
        w_codes = const.tile([P, 2 * F], U32, align_bytes=64)
        w_scales = const.tile([P, 2 * F], U8, align_bytes=64)
        bo_col = const.tile([P, C], F32)
        g2_all = const.tile([P, D], BF16)

        def interleave(copy, dst, src):
            copy(out=dst.rearrange("p (c i) t -> p c t i", i=4), in_=src.rearrange("p t (c i) -> p c t i", i=4))

        warm_ps = psum1.tile([P, D], F32, name="v_ps")
        for i in range(4):
            nc.tensor.matmul(warm_ps[:], lhsT=ones[:], rhs=zeros[:], start=True, stop=True)
        for t in range(J):
            if t < 3:
                nc.vector.tensor_scalar(out=wide[:, t, :], in0=wob[:, t, :].bitcast(FP8), scalar1=wsc[:, t : t + 1], scalar2=None, op0=ALU.mult)
            else:
                nc.scalar.activation(out=wide[:, t, :], in_=wob[:, t, :].bitcast(FP8), func=ACT.Copy, scale=wsc[:, t : t + 1])

        def ok(u):
            return 0 <= u < NU

        for s in range(-3, NU + 4):
            if ok(s - 2):
                nt_stage(s - 2)
            if ok(s + 3):
                t_stage(s + 3)
            if ok(s - 3):
                sl_stage(s - 3)
            if ok(s - 2):
                nc_stage(s - 2)
            if ok(s + 2):
                qa_stage(s + 2)
            if ok(s - 1):
                r_stage(s - 1)
            if ok(s):
                x_stage(s)
                sq_stage(s)
            if s == -3:
                interleave(nc.vector.tensor_copy, wo_g[:, 0:CUT, :], wide[:, :, 0:CUT])
                interleave(nc.scalar.copy, wo_g[:, CUT:D, :], wide[:, :, CUT:D])
                nc.vector.quantize_mx(out=wo_codes[:].bitcast(FP8X4), scales=wo_scales[:], in_=wo_g[:].rearrange("p n j -> p (n j)"))
                bo_ps = psum1.tile([P, P], F32, name="nT_ps")
                nc.tensor.matmul(bo_ps[:], lhsT=bo_rows[:], rhs=ident_bf[:], start=True, stop=True)
                nc.scalar.copy(out=bo_col[:], in_=bo_ps[:, 0:C])
            if ok(s + 2):
                yt_stage(s + 2)
            if ok(s + 3):
                c_stage(s + 3)
            if s == -1:
                g2_ps = psum1.tile([P, D], F32, name="u_ps")
                nc.tensor.matmul(g2_ps[:], lhsT=ones[:], rhs=g2_row[:], start=True, stop=True)
                nc.scalar.copy(out=g2_all[:], in_=g2_ps[:])
            if ok(s + 1):
                yk_stage(s + 1)
            if s == 0:
                interleave(nc.vector.tensor_copy, w_g[:, 0:F, :], w_raw1[:])
                interleave(nc.vector.tensor_copy, w_g[:, F : 2 * F, :], w_raw3[:])
            if ok(s - 3):
                ml_stage(s - 3)
            if ok(s + 2):
                ybv_stage(s + 2)
                yb_stage(s + 2)
            if ok(s - 2):
                qn_stage(s - 2)
            if s == 1:
                nc.vector.quantize_mx(out=w_codes[:].bitcast(FP8X4), scales=w_scales[:], in_=w_g[:].rearrange("p n j -> p (n j)"))
            if ok(s - 1):
                n_stage(s - 1)
            if ok(s - 2):
                uv_stage(s - 2)
